import numpy as np
import ml_dtypes


def mxq(x, axis, fmt="e4m3"):
    dtype, down = {"e4m3": (ml_dtypes.float8_e4m3fn, 7), "e5m2": (ml_dtypes.float8_e5m2, 14)}[fmt]
    v = np.moveaxis(np.asarray(x, np.float32).astype(ml_dtypes.bfloat16).astype(np.float64), axis, -1)
    blocks = v.reshape(v.shape[:-1] + (-1, 32))
    amax = np.abs(blocks).max(-1, keepdims=True)
    byte = np.maximum(np.where(amax > 0, np.frexp(amax)[1] - 1 + 127, 0) - down, 1)
    scale = np.exp2(byte - 127.0)
    codes = (blocks / scale).astype(np.float32).astype(dtype).astype(np.float64)
    return np.moveaxis((codes * scale).reshape(v.shape), -1, axis)


WIDE = False


def mx_kscale(k):
    if not WIDE:
        return np.ones(k)
    levels = np.array([10, -10, 5, -5, 0])
    a = np.random.permutation(np.resize(levels, k // 512 * 4)).reshape(k // 512, 4)
    idx = np.arange(k)
    return np.exp2(a[idx // 512, idx % 128 // 32])


BF16 = ml_dtypes.bfloat16


def bf(x):
    return np.asarray(x, np.float32).astype(BF16)


def f64(x):
    return np.asarray(x).astype(np.float64)


E2M1 = np.array([0.0, 0.5, 1.0, 1.5, 2.0, 3.0, 4.0, 6.0, -0.0, -0.5, -1.0, -1.5, -2.0, -3.0, -4.0, -6.0])


def pack_weight(w, fmt):
    k, n = w.shape
    w = f64(bf(w)).reshape(k // 32, 32, n)
    amax = np.abs(w).max(1)
    if fmt == "e4m3":
        byte = np.frexp(amax)[1] - 1 + 127 - 7
    else:
        mant, ex = np.frexp(amax / 6.0)
        byte = np.where(mant > 0.5, ex, ex - 1) + 127
    byte = np.clip(np.where(amax > 0, byte, 1), 1, 254)
    scaled = (w * np.exp2(127.0 - byte)[:, None, :]).reshape(k, n).astype(np.float32)
    by_word = np.ascontiguousarray(scaled.reshape(k // 512, 128, 4, n).transpose(0, 1, 3, 2))
    if fmt == "e4m3":
        words = by_word.astype(ml_dtypes.float8_e4m3fn).view(np.uint8)
    else:
        c = by_word.astype(ml_dtypes.float4_e2m1fn).view(np.uint8) & 0xF
        words = c[..., 0::2] | (c[..., 1::2] << 4)
    return np.ascontiguousarray(words), np.ascontiguousarray(byte.astype(np.uint8).reshape(k // 512, 16, n))


def unpack_weight(words, scales, fmt):
    g, p, n, _ = words.shape
    if fmt == "e4m3":
        vals = np.ascontiguousarray(words).view(ml_dtypes.float8_e4m3fn).astype(np.float64)
    else:
        nib = np.empty((g, p, n, 4), np.uint8)
        nib[..., 0::2] = words & 0xF
        nib[..., 1::2] = words >> 4
        vals = E2M1[nib]
    vals = vals * np.repeat(np.exp2(scales.astype(np.float64) - 127.0), 8, axis=1)[..., None]
    return vals.transpose(0, 1, 3, 2).reshape(g * 512, n)

def pack4(w):
    words, scales = pack_weight(w, "e2m1")
    return words.reshape(words.shape[0], 128, -1), scales


def unpack4(words, scales):
    return unpack_weight(words.reshape(words.shape[0], 128, -1, 2), scales, "e2m1")


B, S, D, P, N1, N2, N3 = 4, 1024, 1024, 128, 2, 1, 1
H = N1 + N2 + N3
H1 = N2 + N3


def setup_inputs():
    s = mx_kscale(D)
    a = 1.0 / np.sqrt(D)
    x = bf(np.random.standard_normal((B, S, D)) * s)
    w_now = np.random.standard_normal((H, P, D)) * a / s
    w_back1 = np.random.standard_normal((N2 + N3, P, D)) * a / s
    w_back2 = np.random.standard_normal((N3, P, D)) * a / s
    bias = bf(np.random.standard_normal((H, P)) * 0.5)
    w_now_words, w_now_scales = pack4(w_now.swapaxes(1, 2).reshape(-1, P))
    w_back1_words, w_back1_scales = pack4(w_back1.swapaxes(1, 2).reshape(-1, P))
    w_back2_words, w_back2_scales = pack4(w_back2.swapaxes(1, 2).reshape(-1, P))
    return {"x": x,
            "w_now_words": w_now_words, "w_now_scales": w_now_scales,
            "w_back1_words": w_back1_words, "w_back1_scales": w_back1_scales,
            "w_back2_words": w_back2_words, "w_back2_scales": w_back2_scales,
            "bias": bias}


def reference(x, w_now_words, w_now_scales, w_back1_words, w_back1_scales, w_back2_words, w_back2_scales, bias):
    xq = mxq(f64(x), 2, "e4m3")
    w_now = unpack4(w_now_words, w_now_scales).reshape(H, D, P).swapaxes(1, 2)
    w_back1 = unpack4(w_back1_words, w_back1_scales).reshape(H1, D, P).swapaxes(1, 2)
    w_back2 = unpack4(w_back2_words, w_back2_scales).reshape(N3, D, P).swapaxes(1, 2)
    y = 0.0
    for j, w in enumerate((w_now, w_back1, w_back2)):
        z = xq @ w.reshape(-1, D).T
        y = y + np.pad(z[:, :S - j], ((0, 0), (j, 0), (H * P - z.shape[-1], 0)))
    return y.reshape(B, S, H, P).transpose(0, 2, 1, 3) + f64(bias)[None, :, None, :]

@@ -1,0 +1,197 @@
+from contextlib import ExitStack
+
+import concourse.mybir as mybir
+from concourse.masks import make_identity
+
+F32 = mybir.dt.float32
+BF16 = mybir.dt.bfloat16
+I32 = mybir.dt.int32
+U32 = mybir.dt.uint32
+U8 = mybir.dt.uint8
+FP8X4 = mybir.dt.float8_e4m3fn_x4
+FP4X4 = mybir.dt.float4_e2m1fn_x4
+
+P = 128
+BATCH, SEQ, DIM = 4, 1024, 1024
+HEADS, WIDTH = 4, 128
+STEPS = BATCH * SEQ // P
+CHUNKS = SEQ // STEPS
+PACK = 4
+K_PASS = P * PACK
+HALVES = DIM // K_PASS
+WORDS = K_PASS // 2
+ROUND = 4
+N_ROUNDS = STEPS // ROUND
+TAPS = 7
+FP4_BYTES = 2 * WIDTH
+
+FLOPS = 2 * BATCH * SEQ * DIM * WIDTH * TAPS
+
+
+def load_scale_rows(nc, planes, scales):
+    rows = scales.rearrange("a q n -> q a n")
+    for quadrant in range(4):
+        nc.sync.dma_start(
+            out=planes[32 * quadrant : 32 * quadrant + 4].bitcast(I32),
+            in_=rows[4 * quadrant : 4 * quadrant + 4].bitcast(I32),
+        )
+
+
+def tile_multiheadhomogeneousattention_pa_t_e_kernel(
+    tc, x, w_now_words, w_now_scales, w_back1_words, w_back1_scales, w_back2_words, w_back2_scales, bias, out
+):
+    nc = tc.nc
+    x_chunks = x.rearrange("n (c r) k -> c n (r k)", r=STEPS)
+    y_chunks = out.rearrange("n h (c r) q -> h c n (r q)", r=STEPS)
+
+    with ExitStack() as ctx:
+        ctx.enter_context(tc.manual_schedule())
+        consts = ctx.enter_context(tc.tile_pool(name="consts", bufs=1))
+        x_pool = ctx.enter_context(tc.tile_pool(name="x", bufs=N_ROUNDS))
+        grouped_pool = ctx.enter_context(tc.tile_pool(name="grouped", bufs=3))
+        quant_pool = ctx.enter_context(tc.tile_pool(name="quant", bufs=N_ROUNDS))
+        y_pool = ctx.enter_context(tc.tile_pool(name="y", bufs=3))
+        flip_pool = ctx.enter_context(tc.psum_pool(name="flip", bufs=ROUND))
+        acc_pool = ctx.enter_context(tc.psum_pool(name="acc", bufs=ROUND))
+
+        load_order = [N_ROUNDS - 1] + list(range(N_ROUNDS - 1))
+        x_rounds = {}
+        for i in load_order:
+            x_round = x_pool.tile([P, ROUND, DIM], BF16)
+            x_rounds[i] = x_round
+
+        def load_x(queue, i):
+            queue.dma_start(
+                out=x_rounds[i][:].rearrange("p j k -> p (j k)"),
+                in_=x_chunks[:, :, i * ROUND * DIM : (i + 1) * ROUND * DIM],
+            )
+
+        load_x(nc.sync, load_order[0])
+
+        identity = consts.tile([P, P], F32)
+        make_identity(nc, identity[:])
+        for i in load_order[1:]:
+            load_x(nc.gpsimd, i)
+
+        planes = consts.tile([P, 14, WIDTH], U8, align_bytes=64)
+        nc.vector.memset(planes[:].bitcast(I32), 0)
+        back1_planes = planes[:, 8:12, :]
+        back2_planes = planes[:, 12:14, :]
+
+        now_words = consts.tile([P, HALVES, HEADS, FP4_BYTES], U8, align_bytes=64)
+        now_planes = consts.tile([P, HALVES, HEADS, WIDTH], U8, align_bytes=64)
+        back1_words = consts.tile([P, 2 * HALVES, FP4_BYTES], U8, align_bytes=64)
+        back2_words = consts.tile([P, HALVES, FP4_BYTES], U8, align_bytes=64)
+
+        load_scale_rows(nc, planes[:, 0:8, :], w_now_scales)
+        now_by_half = w_now_words.rearrange("(e g) p b -> g p e b", g=HALVES)
+        for g in range(HALVES):
+            nc.sync.dma_start(out=now_words[:, g].bitcast(I32), in_=now_by_half[g].bitcast(I32))
+        nc.sync.dma_start(out=back1_words[:].bitcast(I32), in_=w_back1_words.rearrange("a p b -> p a b").bitcast(I32))
+        load_scale_rows(nc, back1_planes, w_back1_scales)
+        nc.sync.dma_start(out=back2_words[:].bitcast(I32), in_=w_back2_words.rearrange("a p b -> p a b").bitcast(I32))
+        load_scale_rows(nc, back2_planes, w_back2_scales)
+
+        bias_rows = consts.tile([P, HEADS * WIDTH], BF16)
+        nc.vector.memset(bias_rows[:], 0.0)
+        nc.scalar.dma_start(out=bias_rows[0:1, :], in_=bias.rearrange("h q -> (h q)").unsqueeze(0))
+        ones = consts.tile([P, P], BF16)
+        nc.vector.memset(ones[:], 1.0)
+
+        moved_grouped = consts.tile([P, 2, HALVES, P, PACK], BF16, align_bytes=64)
+        nc.vector.memset(moved_grouped[:], 0.0)
+        moved_codes = consts.tile([P, 2, HALVES * P], U32, align_bytes=64)
+        moved_scales = consts.tile([P, 2, HALVES * P], U8, align_bytes=64)
+
+        x_codes = {}
+        x_scales = {}
+
+        def quantise(step, grouped, codes, scales):
+            nc.vector.quantize_mx(
+                out=codes.bitcast(FP8X4), scales=scales, in_=grouped.rearrange("p g m t -> p (g m t)")
+            )
+            x_codes[step] = codes
+            x_scales[step] = scales
+
+        def prepare(i):
+            words = x_rounds[i][:].bitcast(F32)
+            grouped = grouped_pool.tile([P, ROUND, HALVES, P, PACK], BF16, align_bytes=64)
+            codes = quant_pool.tile([P, ROUND, HALVES * P], U32, align_bytes=64)
+            scales = quant_pool.tile([P, ROUND, HALVES * P], U8, align_bytes=64)
+            for j in range(ROUND):
+                step = i * ROUND + j
+                flipped = flip_pool.tile([P, HALVES, 2, P], F32)
+                for g in range(HALVES):
+                    for u in range(2):
+                        nc.tensor.transpose(
+                            flipped[:, g, u, :], words[:, j, WORDS * g + u : WORDS * (g + 1) : 2], identity[:]
+                        )
+                paired = flipped[:].rearrange("p g u m -> p g m u")
+                nc.scalar.copy(out=grouped[:, j].bitcast(F32), in_=paired)
+                quantise(step, grouped[:, j], codes[:, j, :], scales[:, j, :])
+                if step >= STEPS - 2:
+                    late = step - (STEPS - 2)
+                    nc.scalar.copy(
+                        out=moved_grouped[:, late, :, BATCH:P, :].bitcast(F32), in_=paired[:, :, 0 : P - BATCH, :]
+                    )
+                    quantise(step - STEPS, moved_grouped[:, late], moved_codes[:, late, :], moved_scales[:, late, :])
+
+        def mx_pass(acc, step, g, words, plane, start, stop):
+            token_cols = slice(g * P, (g + 1) * P)
+            nc.tensor.matmul_mx(
+                out=acc,
+                lhsT=x_codes[step][:, token_cols].bitcast(FP8X4),
+                lhsT_scale=x_scales[step][:, token_cols],
+                rhs=words.bitcast(FP4X4),
+                rhs_scale=plane,
+                start=start,
+                stop=stop,
+            )
+
+        def multiply(i):
+            y_round = y_pool.tile([P, HEADS, ROUND, WIDTH], F32)
+            for j in range(ROUND):
+                step = i * ROUND + j
+                acc = acc_pool.tile([P, HEADS, WIDTH], F32)
+                everything = acc[:].rearrange("p h q -> p (h q)")
+                mx_pass(
+                    everything, step, 0, now_words[:, 0].rearrange("p e b -> p (e b)"),
+                    now_planes[:, 0].rearrange("p e n -> p (e n)"), True, False,
+                )
+                for g in range(HALVES):
+                    for e in range(2):
+                        mx_pass(
+                            acc[:, 2 + e, :], step - 1, g, back1_words[:, HALVES * e + g, :],
+                            back1_planes[:, HALVES * e + g, :], False, False,
+                        )
+                for g in range(HALVES):
+                    mx_pass(acc[:, 3, :], step - 2, g, back2_words[:, g, :], back2_planes[:, g, :], False, False)
+                mx_pass(
+                    everything, step, 1, now_words[:, 1].rearrange("p e b -> p (e b)"),
+                    now_planes[:, 1].rearrange("p e n -> p (e n)"), False, True,
+                )
+                nc.vector.tensor_tensor(out=y_round[:, :, j, :], in0=acc[:], in1=bias_all[:], op=mybir.AluOpType.add)
+            for h in range(HEADS):
+                nc.sync.dma_start(
+                    out=y_chunks[h, :, :, i * ROUND * WIDTH : (i + 1) * ROUND * WIDTH],
+                    in_=y_round[:, h].rearrange("p j q -> p (j q)"),
+                )
+
+        prepare(N_ROUNDS - 1)
+        prepare(0)
+
+        nc.vector.tensor_copy(
+            out=now_planes[:].bitcast(I32),
+            in_=planes[:, 0:8, :].bitcast(I32).rearrange("p (e g) w -> p g e w", g=HALVES),
+        )
+        bias_bank = acc_pool.tile([P, HEADS, WIDTH], F32, tag="acc")
+        nc.tensor.matmul(
+            out=bias_bank[:].rearrange("p h q -> p (h q)"), lhsT=ones[:], rhs=bias_rows[:], start=True, stop=True
+        )
+        bias_all = consts.tile([P, HEADS, WIDTH], F32)
+        nc.vector.tensor_copy(out=bias_all[:], in_=bias_bank[:])
+
+        for i in range(N_ROUNDS):
+            if i + 1 < N_ROUNDS - 1:
+                prepare(i + 1)
+            multiply(i)

@@ -47,36 +47,39 @@ def tile_multiheadhomogeneousattention_pa_t_e_kernel(
     with ExitStack() as ctx:
         ctx.enter_context(tc.manual_schedule())
         consts = ctx.enter_context(tc.tile_pool(name="consts", bufs=1))
-        x_pool = ctx.enter_context(tc.tile_pool(name="x", bufs=N_ROUNDS))
+        x_pool = ctx.enter_context(tc.tile_pool(name="x", bufs=1))
         grouped_pool = ctx.enter_context(tc.tile_pool(name="grouped", bufs=3))
         quant_pool = ctx.enter_context(tc.tile_pool(name="quant", bufs=N_ROUNDS))
         y_pool = ctx.enter_context(tc.tile_pool(name="y", bufs=3))
         flip_pool = ctx.enter_context(tc.psum_pool(name="flip", bufs=ROUND))
         acc_pool = ctx.enter_context(tc.psum_pool(name="acc", bufs=ROUND))
 
-        load_order = [N_ROUNDS - 1] + list(range(N_ROUNDS - 1))
-        x_rounds = {}
-        for i in load_order:
-            x_round = x_pool.tile([P, ROUND, DIM], BF16)
-            x_rounds[i] = x_round
-
-        def load_x(queue, i):
-            queue.dma_start(
-                out=x_rounds[i][:].rearrange("p j k -> p (j k)"),
-                in_=x_chunks[:, :, i * ROUND * DIM : (i + 1) * ROUND * DIM],
-            )
-
-        load_x(nc.sync, load_order[0])
-
-        identity = consts.tile([P, P], F32)
-        make_identity(nc, identity[:])
-        for i in load_order[1:]:
-            load_x(nc.gpsimd, i)
-
         planes = consts.tile([P, 14, WIDTH], U8, align_bytes=64)
         nc.vector.memset(planes[:].bitcast(I32), 0)
         back1_planes = planes[:, 8:12, :]
         back2_planes = planes[:, 12:14, :]
+
+        bias_rows = consts.tile([P, HEADS * WIDTH], BF16)
+        nc.vector.memset(bias_rows[:], 0.0)
+        nc.scalar.dma_start(out=bias_rows[0:1, :], in_=bias.rearrange("h q -> (h q)").unsqueeze(0))
+
+        x_words = {}
+
+        def load_x(first, count):
+            x_piece = x_pool.tile([P, count, DIM], BF16, name="x%d" % first)
+            nc.gpsimd.dma_start(
+                out=x_piece[:].rearrange("p j k -> p (j k)"),
+                in_=x_chunks[:, :, first * DIM : (first + count) * DIM],
+            )
+            for j in range(count):
+                x_words[first + j] = x_piece[:, j, :].bitcast(F32)
+
+        load_x(0, 2)
+        load_x(2, 2)
+        identity = consts.tile([P, P], F32)
+        make_identity(nc, identity[:])
+        for i in range(1, N_ROUNDS):
+            load_x(i * ROUND, ROUND)
 
         now_words = consts.tile([P, HALVES, HEADS, FP4_BYTES], U8, align_bytes=64)
         now_planes = consts.tile([P, HALVES, HEADS, WIDTH], U8, align_bytes=64)
@@ -92,9 +95,6 @@ def tile_multiheadhomogeneousattention_pa_t_e_kernel(
         nc.sync.dma_start(out=back2_words[:].bitcast(I32), in_=w_back2_words.rearrange("a p b -> p a b").bitcast(I32))
         load_scale_rows(nc, back2_planes, w_back2_scales)
 
-        bias_rows = consts.tile([P, HEADS * WIDTH], BF16)
-        nc.vector.memset(bias_rows[:], 0.0)
-        nc.scalar.dma_start(out=bias_rows[0:1, :], in_=bias.rearrange("h q -> (h q)").unsqueeze(0))
         ones = consts.tile([P, P], BF16)
         nc.vector.memset(ones[:], 1.0)
 
@@ -114,7 +114,6 @@ def tile_multiheadhomogeneousattention_pa_t_e_kernel(
             x_scales[step] = scales
 
         def prepare(i):
-            words = x_rounds[i][:].bitcast(F32)
             grouped = grouped_pool.tile([P, ROUND, HALVES, P, PACK], BF16, align_bytes=64)
             codes = quant_pool.tile([P, ROUND, HALVES * P], U32, align_bytes=64)
             scales = quant_pool.tile([P, ROUND, HALVES * P], U8, align_bytes=64)
@@ -124,7 +123,7 @@ def tile_multiheadhomogeneousattention_pa_t_e_kernel(
                 for g in range(HALVES):
                     for u in range(2):
                         nc.tensor.transpose(
-                            flipped[:, g, u, :], words[:, j, WORDS * g + u : WORDS * (g + 1) : 2], identity[:]
+                            flipped[:, g, u, :], x_words[step][:, WORDS * g + u : WORDS * (g + 1) : 2], identity[:]
                         )
                 paired = flipped[:].rearrange("p g u m -> p g m u")
                 nc.scalar.copy(out=grouped[:, j].bitcast(F32), in_=paired)
@@ -148,10 +147,10 @@ def tile_multiheadhomogeneousattention_pa_t_e_kernel(
                 stop=stop,
             )
 
-        def multiply(i):
-            y_round = y_pool.tile([P, HEADS, ROUND, WIDTH], F32)
-            for j in range(ROUND):
-                step = i * ROUND + j
+        def multiply(first, count):
+            y_round = y_pool.tile([P, HEADS, count, WIDTH], F32)
+            for j in range(count):
+                step = first + j
                 acc = acc_pool.tile([P, HEADS, WIDTH], F32)
                 everything = acc[:].rearrange("p h q -> p (h q)")
                 mx_pass(
@@ -173,12 +172,12 @@ def tile_multiheadhomogeneousattention_pa_t_e_kernel(
                 nc.vector.tensor_tensor(out=y_round[:, :, j, :], in0=acc[:], in1=bias_all[:], op=mybir.AluOpType.add)
             for h in range(HEADS):
                 nc.sync.dma_start(
-                    out=y_chunks[h, :, :, i * ROUND * WIDTH : (i + 1) * ROUND * WIDTH],
+                    out=y_chunks[h, :, :, first * WIDTH : (first + count) * WIDTH],
                     in_=y_round[:, h].rearrange("p j q -> p (j q)"),
                 )
 
-        prepare(N_ROUNDS - 1)
         prepare(0)
+        prepare(1)
 
         nc.vector.tensor_copy(
             out=now_planes[:].bitcast(I32),
@@ -191,7 +190,9 @@ def tile_multiheadhomogeneousattention_pa_t_e_kernel(
         bias_all = consts.tile([P, HEADS, WIDTH], F32)
         nc.vector.tensor_copy(out=bias_all[:], in_=bias_bank[:])
 
-        for i in range(N_ROUNDS):
-            if i + 1 < N_ROUNDS - 1:
+        multiply(2, 2)
+        for i in range(1, N_ROUNDS):
+            if i + 1 < N_ROUNDS:
                 prepare(i + 1)
-            multiply(i)
+            multiply(i * ROUND, ROUND)
+        multiply(0, 2)

@@ -54,52 +54,61 @@ def tile_multiheadhomogeneousattention_pa_t_e_kernel(
         flip_pool = ctx.enter_context(tc.psum_pool(name="flip", bufs=ROUND))
         acc_pool = ctx.enter_context(tc.psum_pool(name="acc", bufs=ROUND))
 
+        x_words = {}
+
+        def load_x(queue, i):
+            x_round = x_pool.tile([P, ROUND, DIM], BF16, name="x%d" % i)
+            queue.dma_start(
+                out=x_round[:].rearrange("p j k -> p (j k)"),
+                in_=x_chunks[:, :, i * ROUND * DIM : (i + 1) * ROUND * DIM],
+            )
+            for j in range(ROUND):
+                x_words[i * ROUND + j] = x_round[:, j, :].bitcast(F32)
+
         planes = consts.tile([P, 14, WIDTH], U8, align_bytes=64)
         nc.vector.memset(planes[:].bitcast(I32), 0)
         back1_planes = planes[:, 8:12, :]
         back2_planes = planes[:, 12:14, :]
 
-        bias_rows = consts.tile([P, HEADS * WIDTH], BF16)
-        nc.vector.memset(bias_rows[:], 0.0)
-        nc.scalar.dma_start(out=bias_rows[0:1, :], in_=bias.rearrange("h q -> (h q)").unsqueeze(0))
-
-        x_words = {}
-
-        def load_x(first, count):
-            x_piece = x_pool.tile([P, count, DIM], BF16, name="x%d" % first)
-            nc.gpsimd.dma_start(
-                out=x_piece[:].rearrange("p j k -> p (j k)"),
-                in_=x_chunks[:, :, first * DIM : (first + count) * DIM],
-            )
-            for j in range(count):
-                x_words[first + j] = x_piece[:, j, :].bitcast(F32)
-
-        load_x(0, 2)
-        load_x(2, 2)
+        load_x(nc.sync, 0)
         identity = consts.tile([P, P], F32)
         make_identity(nc, identity[:])
-        for i in range(1, N_ROUNDS):
-            load_x(i * ROUND, ROUND)
+        load_x(nc.gpsimd, 1)
 
+        bias_rows = consts.tile([P, HEADS * WIDTH], BF16)
+        nc.vector.memset(bias_rows[:], 0.0)
+        nc.gpsimd.dma_start(out=bias_rows[0:1, :], in_=bias.rearrange("h q -> (h q)").unsqueeze(0))
+        ones = consts.tile([P, P], BF16)
+        nc.vector.memset(ones[:], 1.0)
+
+        table_warmer = consts.tile([P, 1], BF16)
+        nc.scalar.copy(out=table_warmer[:], in_=ones[:, 0:1])
+
+        now_words_raw = consts.tile([P, HEADS * HALVES, FP4_BYTES], U8, align_bytes=64)
         now_words = consts.tile([P, HALVES, HEADS, FP4_BYTES], U8, align_bytes=64)
         now_planes = consts.tile([P, HALVES, HEADS, WIDTH], U8, align_bytes=64)
         back1_words = consts.tile([P, 2 * HALVES, FP4_BYTES], U8, align_bytes=64)
         back2_words = consts.tile([P, HALVES, FP4_BYTES], U8, align_bytes=64)
 
         load_scale_rows(nc, planes[:, 0:8, :], w_now_scales)
-        now_by_half = w_now_words.rearrange("(e g) p b -> g p e b", g=HALVES)
-        for g in range(HALVES):
-            nc.sync.dma_start(out=now_words[:, g].bitcast(I32), in_=now_by_half[g].bitcast(I32))
+        nc.sync.dma_start(out=now_words_raw[:].bitcast(I32), in_=w_now_words.rearrange("a p b -> p a b").bitcast(I32))
         nc.sync.dma_start(out=back1_words[:].bitcast(I32), in_=w_back1_words.rearrange("a p b -> p a b").bitcast(I32))
-        load_scale_rows(nc, back1_planes, w_back1_scales)
         nc.sync.dma_start(out=back2_words[:].bitcast(I32), in_=w_back2_words.rearrange("a p b -> p a b").bitcast(I32))
+        load_scale_rows(nc, back1_planes, w_back1_scales)
         load_scale_rows(nc, back2_planes, w_back2_scales)
+        for i in range(2, N_ROUNDS):
+            load_x(nc.sync, i)
 
-        ones = consts.tile([P, P], BF16)
-        nc.vector.memset(ones[:], 1.0)
+        nc.vector.tensor_copy(
+            out=now_words[:].bitcast(I32),
+            in_=now_words_raw[:].bitcast(I32).rearrange("p (e g) w -> p g e w", g=HALVES),
+        )
+        nc.vector.tensor_copy(
+            out=now_planes[:].bitcast(I32),
+            in_=planes[:, 0:8, :].bitcast(I32).rearrange("p (e g) w -> p g e w", g=HALVES),
+        )
 
         moved_grouped = consts.tile([P, 2, HALVES, P, PACK], BF16, align_bytes=64)
-        nc.vector.memset(moved_grouped[:], 0.0)
         moved_codes = consts.tile([P, 2, HALVES * P], U32, align_bytes=64)
         moved_scales = consts.tile([P, 2, HALVES * P], U8, align_bytes=64)
 
@@ -179,16 +188,13 @@ def tile_multiheadhomogeneousattention_pa_t_e_kernel(
         prepare(0)
         prepare(1)
 
-        nc.vector.tensor_copy(
-            out=now_planes[:].bitcast(I32),
-            in_=planes[:, 0:8, :].bitcast(I32).rearrange("p (e g) w -> p g e w", g=HALVES),
-        )
         bias_bank = acc_pool.tile([P, HEADS, WIDTH], F32, tag="acc")
         nc.tensor.matmul(
             out=bias_bank[:].rearrange("p h q -> p (h q)"), lhsT=ones[:], rhs=bias_rows[:], start=True, stop=True
         )
         bias_all = consts.tile([P, HEADS, WIDTH], F32)
         nc.vector.tensor_copy(out=bias_all[:], in_=bias_bank[:])
+        nc.vector.memset(moved_grouped[:], 0.0)
 
         multiply(2, 2)
         for i in range(1, N_ROUNDS):

@@ -22,6 +22,7 @@ HALVES = DIM // K_PASS
 WORDS = K_PASS // 2
 ROUND = 4
 N_ROUNDS = STEPS // ROUND
+FIRST_SORTED = 3
 TAPS = 7
 FP4_BYTES = 2 * WIDTH
 
@@ -48,6 +49,7 @@ def tile_multiheadhomogeneousattention_pa_t_e_kernel(
         ctx.enter_context(tc.manual_schedule())
         consts = ctx.enter_context(tc.tile_pool(name="consts", bufs=1))
         x_pool = ctx.enter_context(tc.tile_pool(name="x", bufs=1))
+        sorted_pool = ctx.enter_context(tc.tile_pool(name="sorted", bufs=2))
         grouped_pool = ctx.enter_context(tc.tile_pool(name="grouped", bufs=3))
         quant_pool = ctx.enter_context(tc.tile_pool(name="quant", bufs=N_ROUNDS))
         y_pool = ctx.enter_context(tc.tile_pool(name="y", bufs=3))
@@ -55,6 +57,7 @@ def tile_multiheadhomogeneousattention_pa_t_e_kernel(
         acc_pool = ctx.enter_context(tc.psum_pool(name="acc", bufs=ROUND))
 
         x_words = {}
+        x_rounds = {}
 
         def load_x(queue, i):
             x_round = x_pool.tile([P, ROUND, DIM], BF16, name="x%d" % i)
@@ -62,6 +65,7 @@ def tile_multiheadhomogeneousattention_pa_t_e_kernel(
                 out=x_round[:].rearrange("p j k -> p (j k)"),
                 in_=x_chunks[:, :, i * ROUND * DIM : (i + 1) * ROUND * DIM],
             )
+            x_rounds[i] = x_round
             for j in range(ROUND):
                 x_words[i * ROUND + j] = x_round[:, j, :].bitcast(F32)
 
@@ -122,6 +126,15 @@ def tile_multiheadhomogeneousattention_pa_t_e_kernel(
             x_codes[step] = codes
             x_scales[step] = scales
 
+        sorted_words = {}
+
+        def sort_words(i):
+            in_order = sorted_pool.tile([P, ROUND * HALVES, 2, P], F32)
+            as_loaded = x_rounds[i][:].rearrange("p j k -> p (j k)").bitcast(F32)
+            nc.scalar.copy(out=in_order[:], in_=as_loaded.rearrange("p (a q u) -> p a u q", q=P, u=2))
+            for j in range(ROUND):
+                sorted_words[i * ROUND + j] = in_order[:, HALVES * j : HALVES * (j + 1)]
+
         def prepare(i):
             grouped = grouped_pool.tile([P, ROUND, HALVES, P, PACK], BF16, align_bytes=64)
             codes = quant_pool.tile([P, ROUND, HALVES * P], U32, align_bytes=64)
@@ -131,9 +144,11 @@ def tile_multiheadhomogeneousattention_pa_t_e_kernel(
                 flipped = flip_pool.tile([P, HALVES, 2, P], F32)
                 for g in range(HALVES):
                     for u in range(2):
-                        nc.tensor.transpose(
-                            flipped[:, g, u, :], x_words[step][:, WORDS * g + u : WORDS * (g + 1) : 2], identity[:]
-                        )
+                        if i >= FIRST_SORTED:
+                            every_second_word = sorted_words[step][:, g, u, :]
+                        else:
+                            every_second_word = x_words[step][:, WORDS * g + u : WORDS * (g + 1) : 2]
+                        nc.tensor.transpose(flipped[:, g, u, :], every_second_word, identity[:])
                 paired = flipped[:].rearrange("p g u m -> p g m u")
                 nc.scalar.copy(out=grouped[:, j].bitcast(F32), in_=paired)
                 quantise(step, grouped[:, j], codes[:, j, :], scales[:, j, :])
@@ -200,5 +215,7 @@ def tile_multiheadhomogeneousattention_pa_t_e_kernel(
         for i in range(1, N_ROUNDS):
             if i + 1 < N_ROUNDS:
                 prepare(i + 1)
+            if FIRST_SORTED <= i + 2 < N_ROUNDS:
+                sort_words(i + 2)
             multiply(i * ROUND, ROUND)
         multiply(0, 2)

@@ -131,7 +131,9 @@ def tile_multiheadhomogeneousattention_pa_t_e_kernel(
         def sort_words(i):
             in_order = sorted_pool.tile([P, ROUND * HALVES, 2, P], F32)
             as_loaded = x_rounds[i][:].rearrange("p j k -> p (j k)").bitcast(F32)
-            nc.scalar.copy(out=in_order[:], in_=as_loaded.rearrange("p (a q u) -> p a u q", q=P, u=2))
+            by_u = as_loaded.rearrange("p (a q u) -> p a u q", q=P, u=2)
+            nc.scalar.copy(out=in_order[:, 0:ROUND], in_=by_u[:, 0:ROUND])
+            nc.vector.tensor_copy(out=in_order[:, ROUND : 2 * ROUND], in_=by_u[:, ROUND : 2 * ROUND])
             for j in range(ROUND):
                 sorted_words[i * ROUND + j] = in_order[:, HALVES * j : HALVES * (j + 1)]
 

@@ -127,39 +127,60 @@ def tile_multiheadhomogeneousattention_pa_t_e_kernel(
             x_scales[step] = scales
 
         sorted_words = {}
+        in_order = {}
+        by_u = {}
+        SCALAR_SHARE = ROUND * HALVES // 2
 
-        def sort_words(i):
-            in_order = sorted_pool.tile([P, ROUND * HALVES, 2, P], F32)
+        def sort_on_scalar(i):
+            sorted_round = sorted_pool.tile([P, ROUND * HALVES, 2, P], F32)
+            in_order[i] = sorted_round
             as_loaded = x_rounds[i][:].rearrange("p j k -> p (j k)").bitcast(F32)
-            by_u = as_loaded.rearrange("p (a q u) -> p a u q", q=P, u=2)
-            nc.scalar.copy(out=in_order[:, 0:ROUND], in_=by_u[:, 0:ROUND])
-            nc.vector.tensor_copy(out=in_order[:, ROUND : 2 * ROUND], in_=by_u[:, ROUND : 2 * ROUND])
+            by_u[i] = as_loaded.rearrange("p (a q u) -> p a u q", q=P, u=2)
+            nc.scalar.copy(out=sorted_round[:, 0:SCALAR_SHARE], in_=by_u[i][:, 0:SCALAR_SHARE])
             for j in range(ROUND):
-                sorted_words[i * ROUND + j] = in_order[:, HALVES * j : HALVES * (j + 1)]
+                sorted_words[i * ROUND + j] = sorted_round[:, HALVES * j : HALVES * (j + 1)]
 
-        def prepare(i):
-            grouped = grouped_pool.tile([P, ROUND, HALVES, P, PACK], BF16, align_bytes=64)
+        def sort_on_vector(i):
+            nc.vector.tensor_copy(out=in_order[i][:, SCALAR_SHARE:], in_=by_u[i][:, SCALAR_SHARE:])
+
+        flipped = {}
+        grouped = {}
+        code_slots = {}
+        scale_slots = {}
+
+        def transpose_round(i):
+            grouped_round = grouped_pool.tile([P, ROUND, HALVES, P, PACK], BF16, align_bytes=64)
             codes = quant_pool.tile([P, ROUND, HALVES * P], U32, align_bytes=64)
             scales = quant_pool.tile([P, ROUND, HALVES * P], U8, align_bytes=64)
             for j in range(ROUND):
                 step = i * ROUND + j
-                flipped = flip_pool.tile([P, HALVES, 2, P], F32)
+                bank = flip_pool.tile([P, HALVES, 2, P], F32)
+                flipped[step] = bank
+                grouped[step] = grouped_round[:, j]
+                code_slots[step] = codes[:, j, :]
+                scale_slots[step] = scales[:, j, :]
                 for g in range(HALVES):
                     for u in range(2):
                         if i >= FIRST_SORTED:
                             every_second_word = sorted_words[step][:, g, u, :]
                         else:
                             every_second_word = x_words[step][:, WORDS * g + u : WORDS * (g + 1) : 2]
-                        nc.tensor.transpose(flipped[:, g, u, :], every_second_word, identity[:])
-                paired = flipped[:].rearrange("p g u m -> p g m u")
-                nc.scalar.copy(out=grouped[:, j].bitcast(F32), in_=paired)
-                quantise(step, grouped[:, j], codes[:, j, :], scales[:, j, :])
-                if step >= STEPS - 2:
-                    late = step - (STEPS - 2)
-                    nc.scalar.copy(
-                        out=moved_grouped[:, late, :, BATCH:P, :].bitcast(F32), in_=paired[:, :, 0 : P - BATCH, :]
-                    )
-                    quantise(step - STEPS, moved_grouped[:, late], moved_codes[:, late, :], moved_scales[:, late, :])
+                        nc.tensor.transpose(bank[:, g, u, :], every_second_word, identity[:])
+
+        def pair_words(step):
+            paired = flipped[step][:].rearrange("p g u m -> p g m u")
+            nc.scalar.copy(out=grouped[step].bitcast(F32), in_=paired)
+            if step >= STEPS - 2:
+                late = step - (STEPS - 2)
+                nc.scalar.copy(
+                    out=moved_grouped[:, late, :, BATCH:P, :].bitcast(F32), in_=paired[:, :, 0 : P - BATCH, :]
+                )
+
+        def quantise_step(step):
+            quantise(step, grouped[step], code_slots[step], scale_slots[step])
+            if step >= STEPS - 2:
+                late = step - (STEPS - 2)
+                quantise(step - STEPS, moved_grouped[:, late], moved_codes[:, late, :], moved_scales[:, late, :])
 
         def mx_pass(acc, step, g, words, plane, start, stop):
             token_cols = slice(g * P, (g + 1) * P)
@@ -173,37 +194,39 @@ def tile_multiheadhomogeneousattention_pa_t_e_kernel(
                 stop=stop,
             )
 
-        def multiply(first, count):
-            y_round = y_pool.tile([P, HEADS, count, WIDTH], F32)
-            for j in range(count):
-                step = first + j
-                acc = acc_pool.tile([P, HEADS, WIDTH], F32)
-                everything = acc[:].rearrange("p h q -> p (h q)")
-                mx_pass(
-                    everything, step, 0, now_words[:, 0].rearrange("p e b -> p (e b)"),
-                    now_planes[:, 0].rearrange("p e n -> p (e n)"), True, False,
-                )
-                for g in range(HALVES):
-                    for e in range(2):
-                        mx_pass(
-                            acc[:, 2 + e, :], step - 1, g, back1_words[:, HALVES * e + g, :],
-                            back1_planes[:, HALVES * e + g, :], False, False,
-                        )
-                for g in range(HALVES):
-                    mx_pass(acc[:, 3, :], step - 2, g, back2_words[:, g, :], back2_planes[:, g, :], False, False)
-                mx_pass(
-                    everything, step, 1, now_words[:, 1].rearrange("p e b -> p (e b)"),
-                    now_planes[:, 1].rearrange("p e n -> p (e n)"), False, True,
-                )
-                nc.vector.tensor_tensor(out=y_round[:, :, j, :], in0=acc[:], in1=bias_all[:], op=mybir.AluOpType.add)
+        def multiply_step(y_round, j, step):
+            acc = acc_pool.tile([P, HEADS, WIDTH], F32)
+            everything = acc[:].rearrange("p h q -> p (h q)")
+            mx_pass(
+                everything, step, 0, now_words[:, 0].rearrange("p e b -> p (e b)"),
+                now_planes[:, 0].rearrange("p e n -> p (e n)"), True, False,
+            )
+            for g in range(HALVES):
+                for e in range(2):
+                    mx_pass(
+                        acc[:, 2 + e, :], step - 1, g, back1_words[:, HALVES * e + g, :],
+                        back1_planes[:, HALVES * e + g, :], False, False,
+                    )
+            for g in range(HALVES):
+                mx_pass(acc[:, 3, :], step - 2, g, back2_words[:, g, :], back2_planes[:, g, :], False, False)
+            mx_pass(
+                everything, step, 1, now_words[:, 1].rearrange("p e b -> p (e b)"),
+                now_planes[:, 1].rearrange("p e n -> p (e n)"), False, True,
+            )
+            nc.vector.tensor_tensor(out=y_round[:, :, j, :], in0=acc[:], in1=bias_all[:], op=mybir.AluOpType.add)
+
+        def store(y_round, first, count):
             for h in range(HEADS):
                 nc.sync.dma_start(
                     out=y_chunks[h, :, :, first * WIDTH : (first + count) * WIDTH],
                     in_=y_round[:, h].rearrange("p j q -> p (j q)"),
                 )
 
-        prepare(0)
-        prepare(1)
+        for i in range(2):
+            transpose_round(i)
+            for j in range(ROUND):
+                pair_words(i * ROUND + j)
+                quantise_step(i * ROUND + j)
 
         bias_bank = acc_pool.tile([P, HEADS, WIDTH], F32, tag="acc")
         nc.tensor.matmul(
@@ -213,11 +236,38 @@ def tile_multiheadhomogeneousattention_pa_t_e_kernel(
         nc.vector.tensor_copy(out=bias_all[:], in_=bias_bank[:])
         nc.vector.memset(moved_grouped[:], 0.0)
 
-        multiply(2, 2)
+        y_round = y_pool.tile([P, HEADS, 2, WIDTH], F32)
+        for j in range(2):
+            multiply_step(y_round, j, 2 + j)
+        store(y_round, 2, 2)
+
         for i in range(1, N_ROUNDS):
-            if i + 1 < N_ROUNDS:
-                prepare(i + 1)
-            if FIRST_SORTED <= i + 2 < N_ROUNDS:
-                sort_words(i + 2)
-            multiply(i * ROUND, ROUND)
-        multiply(0, 2)
+            ahead = i + 1
+            to_sort = i + 2
+            first = i * ROUND
+            y_round = y_pool.tile([P, HEADS, ROUND, WIDTH], F32)
+            if ahead < N_ROUNDS:
+                transpose_round(ahead)
+                for j in range(ROUND):
+                    pair_words(ahead * ROUND + j)
+            if FIRST_SORTED <= to_sort < N_ROUNDS:
+                sort_on_scalar(to_sort)
+            if ahead < N_ROUNDS:
+                quantise_step(ahead * ROUND)
+                quantise_step(ahead * ROUND + 1)
+            multiply_step(y_round, 0, first)
+            if ahead < N_ROUNDS:
+                quantise_step(ahead * ROUND + 2)
+            multiply_step(y_round, 1, first + 1)
+            if ahead < N_ROUNDS:
+                quantise_step(ahead * ROUND + 3)
+            if FIRST_SORTED <= to_sort < N_ROUNDS:
+                sort_on_vector(to_sort)
+            multiply_step(y_round, 2, first + 2)
+            multiply_step(y_round, 3, first + 3)
+            store(y_round, first, ROUND)
+
+        y_round = y_pool.tile([P, HEADS, 2, WIDTH], F32)
+        for j in range(2):
+            multiply_step(y_round, j, j)
+        store(y_round, 0, 2)

@@ -22,7 +22,7 @@ HALVES = DIM // K_PASS
 WORDS = K_PASS // 2
 ROUND = 4
 N_ROUNDS = STEPS // ROUND
-FIRST_SORTED = 3
+FIRST_SORTED = 2
 TAPS = 7
 FP4_BYTES = 2 * WIDTH
 
@@ -82,6 +82,7 @@ def tile_multiheadhomogeneousattention_pa_t_e_kernel(
         bias_rows = consts.tile([P, HEADS * WIDTH], BF16)
         nc.vector.memset(bias_rows[:], 0.0)
         nc.gpsimd.dma_start(out=bias_rows[0:1, :], in_=bias.rearrange("h q -> (h q)").unsqueeze(0))
+        load_x(nc.gpsimd, 2)
         ones = consts.tile([P, P], BF16)
         nc.vector.memset(ones[:], 1.0)
 
@@ -100,7 +101,7 @@ def tile_multiheadhomogeneousattention_pa_t_e_kernel(
         nc.sync.dma_start(out=back2_words[:].bitcast(I32), in_=w_back2_words.rearrange("a p b -> p a b").bitcast(I32))
         load_scale_rows(nc, back1_planes, w_back1_scales)
         load_scale_rows(nc, back2_planes, w_back2_scales)
-        for i in range(2, N_ROUNDS):
+        for i in range(3, N_ROUNDS):
             load_x(nc.sync, i)
 
         nc.vector.tensor_copy(
@@ -227,6 +228,8 @@ def tile_multiheadhomogeneousattention_pa_t_e_kernel(
             for j in range(ROUND):
                 pair_words(i * ROUND + j)
                 quantise_step(i * ROUND + j)
+        sort_on_scalar(FIRST_SORTED)
+        sort_on_vector(FIRST_SORTED)
 
         bias_bank = acc_pool.tile([P, HEADS, WIDTH], F32, tag="acc")
         nc.tensor.matmul(
@@ -250,7 +253,7 @@ def tile_multiheadhomogeneousattention_pa_t_e_kernel(
                 transpose_round(ahead)
                 for j in range(ROUND):
                     pair_words(ahead * ROUND + j)
-            if FIRST_SORTED <= to_sort < N_ROUNDS:
+            if to_sort < N_ROUNDS:
                 sort_on_scalar(to_sort)
             if ahead < N_ROUNDS:
                 quantise_step(ahead * ROUND)
@@ -261,7 +264,7 @@ def tile_multiheadhomogeneousattention_pa_t_e_kernel(
             multiply_step(y_round, 1, first + 1)
             if ahead < N_ROUNDS:
                 quantise_step(ahead * ROUND + 3)
-            if FIRST_SORTED <= to_sort < N_ROUNDS:
+            if to_sort < N_ROUNDS:
                 sort_on_vector(to_sort)
             multiply_step(y_round, 2, first + 2)
             multiply_step(y_round, 3, first + 3)

@@ -22,6 +22,7 @@ HALVES = DIM // K_PASS
 WORDS = K_PASS // 2
 ROUND = 4
 N_ROUNDS = STEPS // ROUND
+WARM_FIRST = 5
 FIRST_SORTED = 2
 TAPS = 7
 FP4_BYTES = 2 * WIDTH
@@ -69,12 +70,24 @@ def tile_multiheadhomogeneousattention_pa_t_e_kernel(
             for j in range(ROUND):
                 x_words[i * ROUND + j] = x_round[:, j, :].bitcast(F32)
 
+        zeros = consts.tile([P, HEADS * WIDTH], BF16)
+        nc.vector.memset(zeros[:], 0.0)
         planes = consts.tile([P, 14, WIDTH], U8, align_bytes=64)
         nc.vector.memset(planes[:].bitcast(I32), 0)
         back1_planes = planes[:, 8:12, :]
         back2_planes = planes[:, 12:14, :]
 
         load_x(nc.sync, 0)
+
+        bias_bank = acc_pool.tile([P, HEADS, WIDTH], F32, tag="acc")
+
+        def idle_matmuls(count):
+            for idle in range(count):
+                nc.tensor.matmul(
+                    out=bias_bank[:].rearrange("p h q -> p (h q)"), lhsT=zeros[:, 0:P], rhs=zeros[:], start=True, stop=True
+                )
+
+        idle_matmuls(WARM_FIRST)
         identity = consts.tile([P, P], F32)
         make_identity(nc, identity[:])
         load_x(nc.gpsimd, 1)
@@ -223,20 +236,21 @@ def tile_multiheadhomogeneousattention_pa_t_e_kernel(
                     in_=y_round[:, h].rearrange("p j q -> p (j q)"),
                 )
 
+        bias_all = consts.tile([P, HEADS, WIDTH], F32)
         for i in range(2):
             transpose_round(i)
+            if i == 0:
+                idle_matmuls(1)
+                nc.tensor.matmul(
+                    out=bias_bank[:].rearrange("p h q -> p (h q)"), lhsT=ones[:], rhs=bias_rows[:], start=True, stop=True
+                )
             for j in range(ROUND):
                 pair_words(i * ROUND + j)
                 quantise_step(i * ROUND + j)
+            if i == 0:
+                nc.vector.tensor_copy(out=bias_all[:], in_=bias_bank[:])
         sort_on_scalar(FIRST_SORTED)
         sort_on_vector(FIRST_SORTED)
-
-        bias_bank = acc_pool.tile([P, HEADS, WIDTH], F32, tag="acc")
-        nc.tensor.matmul(
-            out=bias_bank[:].rearrange("p h q -> p (h q)"), lhsT=ones[:], rhs=bias_rows[:], start=True, stop=True
-        )
-        bias_all = consts.tile([P, HEADS, WIDTH], F32)
-        nc.vector.tensor_copy(out=bias_all[:], in_=bias_bank[:])
         nc.vector.memset(moved_grouped[:], 0.0)
 
         y_round = y_pool.tile([P, HEADS, 2, WIDTH], F32)

@@ -22,7 +22,7 @@ HALVES = DIM // K_PASS
 WORDS = K_PASS // 2
 ROUND = 4
 N_ROUNDS = STEPS // ROUND
-WARM_FIRST = 5
+WARM_FIRST = 3
 FIRST_SORTED = 2
 TAPS = 7
 FP4_BYTES = 2 * WIDTH
@@ -70,6 +70,15 @@ def tile_multiheadhomogeneousattention_pa_t_e_kernel(
             for j in range(ROUND):
                 x_words[i * ROUND + j] = x_round[:, j, :].bitcast(F32)
 
+        def load_x_in_halves(queue, i):
+            for first in (i * ROUND, i * ROUND + 2):
+                x_half = x_pool.tile([P, 2, DIM], BF16, name="xh%d" % first)
+                queue.dma_start(
+                    out=x_half[:].rearrange("p j k -> p (j k)"), in_=x_chunks[:, :, first * DIM : (first + 2) * DIM]
+                )
+                for j in range(2):
+                    x_words[first + j] = x_half[:, j, :].bitcast(F32)
+
         zeros = consts.tile([P, HEADS * WIDTH], BF16)
         nc.vector.memset(zeros[:], 0.0)
         planes = consts.tile([P, 14, WIDTH], U8, align_bytes=64)
@@ -77,7 +86,7 @@ def tile_multiheadhomogeneousattention_pa_t_e_kernel(
         back1_planes = planes[:, 8:12, :]
         back2_planes = planes[:, 12:14, :]
 
-        load_x(nc.sync, 0)
+        load_x_in_halves(nc.sync, 0)
 
         bias_bank = acc_pool.tile([P, HEADS, WIDTH], F32, tag="acc")
 
@@ -90,7 +99,7 @@ def tile_multiheadhomogeneousattention_pa_t_e_kernel(
         idle_matmuls(WARM_FIRST)
         identity = consts.tile([P, P], F32)
         make_identity(nc, identity[:])
-        load_x(nc.gpsimd, 1)
+        load_x_in_halves(nc.gpsimd, 1)
 
         bias_rows = consts.tile([P, HEADS * WIDTH], BF16)
         nc.vector.memset(bias_rows[:], 0.0)
@@ -239,15 +248,14 @@ def tile_multiheadhomogeneousattention_pa_t_e_kernel(
         bias_all = consts.tile([P, HEADS, WIDTH], F32)
         for i in range(2):
             transpose_round(i)
-            if i == 0:
-                idle_matmuls(1)
+            if i == 1:
                 nc.tensor.matmul(
                     out=bias_bank[:].rearrange("p h q -> p (h q)"), lhsT=ones[:], rhs=bias_rows[:], start=True, stop=True
                 )
             for j in range(ROUND):
                 pair_words(i * ROUND + j)
                 quantise_step(i * ROUND + j)
-            if i == 0:
+            if i == 1:
                 nc.vector.tensor_copy(out=bias_all[:], in_=bias_bank[:])
         sort_on_scalar(FIRST_SORTED)
         sort_on_vector(FIRST_SORTED)

@@ -81,7 +81,7 @@ def tile_multiheadhomogeneousattention_pa_t_e_kernel(
 
         zeros = consts.tile([P, HEADS * WIDTH], BF16)
         nc.vector.memset(zeros[:], 0.0)
-        planes = consts.tile([P, 14, WIDTH], U8, align_bytes=64)
+        planes = consts.tile([P, 14, WIDTH], U8, align_bytes=256)
         nc.vector.memset(planes[:].bitcast(I32), 0)
         back1_planes = planes[:, 8:12, :]
         back2_planes = planes[:, 12:14, :]
@@ -111,11 +111,11 @@ def tile_multiheadhomogeneousattention_pa_t_e_kernel(
         table_warmer = consts.tile([P, 1], BF16)
         nc.scalar.copy(out=table_warmer[:], in_=ones[:, 0:1])
 
-        now_words_raw = consts.tile([P, HEADS * HALVES, FP4_BYTES], U8, align_bytes=64)
-        now_words = consts.tile([P, HALVES, HEADS, FP4_BYTES], U8, align_bytes=64)
-        now_planes = consts.tile([P, HALVES, HEADS, WIDTH], U8, align_bytes=64)
-        back1_words = consts.tile([P, 2 * HALVES, FP4_BYTES], U8, align_bytes=64)
-        back2_words = consts.tile([P, HALVES, FP4_BYTES], U8, align_bytes=64)
+        now_words_raw = consts.tile([P, HEADS * HALVES, FP4_BYTES], U8, align_bytes=256)
+        now_words = consts.tile([P, HALVES, HEADS, FP4_BYTES], U8, align_bytes=256)
+        now_planes = consts.tile([P, HALVES, HEADS, WIDTH], U8, align_bytes=256)
+        back1_words = consts.tile([P, 2 * HALVES, FP4_BYTES], U8, align_bytes=256)
+        back2_words = consts.tile([P, HALVES, FP4_BYTES], U8, align_bytes=256)
 
         load_scale_rows(nc, planes[:, 0:8, :], w_now_scales)
         nc.sync.dma_start(out=now_words_raw[:].bitcast(I32), in_=w_now_words.rearrange("a p b -> p a b").bitcast(I32))
@@ -135,9 +135,9 @@ def tile_multiheadhomogeneousattention_pa_t_e_kernel(
             in_=planes[:, 0:8, :].bitcast(I32).rearrange("p (e g) w -> p g e w", g=HALVES),
         )
 
-        moved_grouped = consts.tile([P, 2, HALVES, P, PACK], BF16, align_bytes=64)
-        moved_codes = consts.tile([P, 2, HALVES * P], U32, align_bytes=64)
-        moved_scales = consts.tile([P, 2, HALVES * P], U8, align_bytes=64)
+        moved_grouped = consts.tile([P, 2, HALVES, P, PACK], BF16, align_bytes=256)
+        moved_codes = consts.tile([P, 2, HALVES * P], U32, align_bytes=256)
+        moved_scales = consts.tile([P, 2, HALVES * P], U8, align_bytes=256)
 
         x_codes = {}
         x_scales = {}
@@ -172,9 +172,9 @@ def tile_multiheadhomogeneousattention_pa_t_e_kernel(
         scale_slots = {}
 
         def transpose_round(i):
-            grouped_round = grouped_pool.tile([P, ROUND, HALVES, P, PACK], BF16, align_bytes=64)
-            codes = quant_pool.tile([P, ROUND, HALVES * P], U32, align_bytes=64)
-            scales = quant_pool.tile([P, ROUND, HALVES * P], U8, align_bytes=64)
+            grouped_round = grouped_pool.tile([P, ROUND, HALVES, P, PACK], BF16, align_bytes=256)
+            codes = quant_pool.tile([P, ROUND, HALVES * P], U32, align_bytes=256)
+            scales = quant_pool.tile([P, ROUND, HALVES * P], U8, align_bytes=256)
             for j in range(ROUND):
                 step = i * ROUND + j
                 bank = flip_pool.tile([P, HALVES, 2, P], F32)

@@ -61,7 +61,7 @@ def tile_multiheadhomogeneousattention_pa_t_e_kernel(
         x_rounds = {}
 
         def load_x(queue, i):
-            x_round = x_pool.tile([P, ROUND, DIM], BF16, name="x%d" % i)
+            x_round = x_pool.tile([P, ROUND, DIM], BF16, name="x%d" % i, align_bytes=1024)
             queue.dma_start(
                 out=x_round[:].rearrange("p j k -> p (j k)"),
                 in_=x_chunks[:, :, i * ROUND * DIM : (i + 1) * ROUND * DIM],
@@ -72,7 +72,7 @@ def tile_multiheadhomogeneousattention_pa_t_e_kernel(
 
         def load_x_in_halves(queue, i):
             for first in (i * ROUND, i * ROUND + 2):
-                x_half = x_pool.tile([P, 2, DIM], BF16, name="xh%d" % first)
+                x_half = x_pool.tile([P, 2, DIM], BF16, name="xh%d" % first, align_bytes=1024)
                 queue.dma_start(
                     out=x_half[:].rearrange("p j k -> p (j k)"), in_=x_chunks[:, :, first * DIM : (first + 2) * DIM]
                 )
@@ -81,7 +81,7 @@ def tile_multiheadhomogeneousattention_pa_t_e_kernel(
 
         zeros = consts.tile([P, HEADS * WIDTH], BF16)
         nc.vector.memset(zeros[:], 0.0)
-        planes = consts.tile([P, 14, WIDTH], U8, align_bytes=256)
+        planes = consts.tile([P, 14, WIDTH], U8, align_bytes=1024)
         nc.vector.memset(planes[:].bitcast(I32), 0)
         back1_planes = planes[:, 8:12, :]
         back2_planes = planes[:, 12:14, :]
@@ -97,7 +97,7 @@ def tile_multiheadhomogeneousattention_pa_t_e_kernel(
                 )
 
         idle_matmuls(WARM_FIRST)
-        identity = consts.tile([P, P], F32)
+        identity = consts.tile([P, P], F32, align_bytes=1024)
         make_identity(nc, identity[:])
         load_x_in_halves(nc.gpsimd, 1)
 
@@ -111,11 +111,11 @@ def tile_multiheadhomogeneousattention_pa_t_e_kernel(
         table_warmer = consts.tile([P, 1], BF16)
         nc.scalar.copy(out=table_warmer[:], in_=ones[:, 0:1])
 
-        now_words_raw = consts.tile([P, HEADS * HALVES, FP4_BYTES], U8, align_bytes=256)
-        now_words = consts.tile([P, HALVES, HEADS, FP4_BYTES], U8, align_bytes=256)
-        now_planes = consts.tile([P, HALVES, HEADS, WIDTH], U8, align_bytes=256)
-        back1_words = consts.tile([P, 2 * HALVES, FP4_BYTES], U8, align_bytes=256)
-        back2_words = consts.tile([P, HALVES, FP4_BYTES], U8, align_bytes=256)
+        now_words_raw = consts.tile([P, HEADS * HALVES, FP4_BYTES], U8, align_bytes=1024)
+        now_words = consts.tile([P, HALVES, HEADS, FP4_BYTES], U8, align_bytes=1024)
+        now_planes = consts.tile([P, HALVES, HEADS, WIDTH], U8, align_bytes=1024)
+        back1_words = consts.tile([P, 2 * HALVES, FP4_BYTES], U8, align_bytes=1024)
+        back2_words = consts.tile([P, HALVES, FP4_BYTES], U8, align_bytes=1024)
 
         load_scale_rows(nc, planes[:, 0:8, :], w_now_scales)
         nc.sync.dma_start(out=now_words_raw[:].bitcast(I32), in_=w_now_words.rearrange("a p b -> p a b").bitcast(I32))
@@ -135,9 +135,9 @@ def tile_multiheadhomogeneousattention_pa_t_e_kernel(
             in_=planes[:, 0:8, :].bitcast(I32).rearrange("p (e g) w -> p g e w", g=HALVES),
         )
 
-        moved_grouped = consts.tile([P, 2, HALVES, P, PACK], BF16, align_bytes=256)
-        moved_codes = consts.tile([P, 2, HALVES * P], U32, align_bytes=256)
-        moved_scales = consts.tile([P, 2, HALVES * P], U8, align_bytes=256)
+        moved_grouped = consts.tile([P, 2, HALVES, P, PACK], BF16, align_bytes=1024)
+        moved_codes = consts.tile([P, 2, HALVES * P], U32, align_bytes=1024)
+        moved_scales = consts.tile([P, 2, HALVES * P], U8, align_bytes=1024)
 
         x_codes = {}
         x_scales = {}
@@ -155,7 +155,7 @@ def tile_multiheadhomogeneousattention_pa_t_e_kernel(
         SCALAR_SHARE = ROUND * HALVES // 2
 
         def sort_on_scalar(i):
-            sorted_round = sorted_pool.tile([P, ROUND * HALVES, 2, P], F32)
+            sorted_round = sorted_pool.tile([P, ROUND * HALVES, 2, P], F32, align_bytes=1024)
             in_order[i] = sorted_round
             as_loaded = x_rounds[i][:].rearrange("p j k -> p (j k)").bitcast(F32)
             by_u[i] = as_loaded.rearrange("p (a q u) -> p a u q", q=P, u=2)
@@ -172,9 +172,9 @@ def tile_multiheadhomogeneousattention_pa_t_e_kernel(
         scale_slots = {}
 
         def transpose_round(i):
-            grouped_round = grouped_pool.tile([P, ROUND, HALVES, P, PACK], BF16, align_bytes=256)
-            codes = quant_pool.tile([P, ROUND, HALVES * P], U32, align_bytes=256)
-            scales = quant_pool.tile([P, ROUND, HALVES * P], U8, align_bytes=256)
+            grouped_round = grouped_pool.tile([P, ROUND, HALVES, P, PACK], BF16, align_bytes=1024)
+            codes = quant_pool.tile([P, ROUND, HALVES * P], U32, align_bytes=1024)
+            scales = quant_pool.tile([P, ROUND, HALVES * P], U8, align_bytes=1024)
             for j in range(ROUND):
                 step = i * ROUND + j
                 bank = flip_pool.tile([P, HALVES, 2, P], F32)
@@ -245,7 +245,7 @@ def tile_multiheadhomogeneousattention_pa_t_e_kernel(
                     in_=y_round[:, h].rearrange("p j q -> p (j q)"),
                 )
 
-        bias_all = consts.tile([P, HEADS, WIDTH], F32)
+        bias_all = consts.tile([P, HEADS, WIDTH], F32, align_bytes=1024)
         for i in range(2):
             transpose_round(i)
             if i == 1:
@@ -261,7 +261,7 @@ def tile_multiheadhomogeneousattention_pa_t_e_kernel(
         sort_on_vector(FIRST_SORTED)
         nc.vector.memset(moved_grouped[:], 0.0)
 
-        y_round = y_pool.tile([P, HEADS, 2, WIDTH], F32)
+        y_round = y_pool.tile([P, HEADS, 2, WIDTH], F32, align_bytes=1024)
         for j in range(2):
             multiply_step(y_round, j, 2 + j)
         store(y_round, 2, 2)
@@ -270,7 +270,7 @@ def tile_multiheadhomogeneousattention_pa_t_e_kernel(
             ahead = i + 1
             to_sort = i + 2
             first = i * ROUND
-            y_round = y_pool.tile([P, HEADS, ROUND, WIDTH], F32)
+            y_round = y_pool.tile([P, HEADS, ROUND, WIDTH], F32, align_bytes=1024)
             if ahead < N_ROUNDS:
                 transpose_round(ahead)
                 for j in range(ROUND):
@@ -292,7 +292,7 @@ def tile_multiheadhomogeneousattention_pa_t_e_kernel(
             multiply_step(y_round, 3, first + 3)
             store(y_round, first, ROUND)
 
-        y_round = y_pool.tile([P, HEADS, 2, WIDTH], F32)
+        y_round = y_pool.tile([P, HEADS, 2, WIDTH], F32, align_bytes=1024)
         for j in range(2):
             multiply_step(y_round, j, j)
         store(y_round, 0, 2)

@@ -171,12 +171,14 @@ def tile_multiheadhomogeneousattention_pa_t_e_kernel(
         code_slots = {}
         scale_slots = {}
 
-        def transpose_round(i):
+        def transpose_round(i, in_the_middle=None):
             grouped_round = grouped_pool.tile([P, ROUND, HALVES, P, PACK], BF16, align_bytes=1024)
             codes = quant_pool.tile([P, ROUND, HALVES * P], U32, align_bytes=1024)
             scales = quant_pool.tile([P, ROUND, HALVES * P], U8, align_bytes=1024)
             for j in range(ROUND):
                 step = i * ROUND + j
+                if j == 2 and in_the_middle:
+                    in_the_middle()
                 bank = flip_pool.tile([P, HALVES, 2, P], F32)
                 flipped[step] = bank
                 grouped[step] = grouped_round[:, j]
@@ -246,12 +248,13 @@ def tile_multiheadhomogeneousattention_pa_t_e_kernel(
                 )
 
         bias_all = consts.tile([P, HEADS, WIDTH], F32, align_bytes=1024)
+        def spread_bias():
+            nc.tensor.matmul(
+                out=bias_bank[:].rearrange("p h q -> p (h q)"), lhsT=ones[:], rhs=bias_rows[:], start=True, stop=True
+            )
+
         for i in range(2):
-            transpose_round(i)
-            if i == 1:
-                nc.tensor.matmul(
-                    out=bias_bank[:].rearrange("p h q -> p (h q)"), lhsT=ones[:], rhs=bias_rows[:], start=True, stop=True
-                )
+            transpose_round(i, spread_bias if i == 1 else None)
             for j in range(ROUND):
                 pair_words(i * ROUND + j)
                 quantise_step(i * ROUND + j)

from contextlib import ExitStack

import concourse.mybir as mybir
from concourse.masks import make_identity

F32 = mybir.dt.float32
BF16 = mybir.dt.bfloat16
I32 = mybir.dt.int32
U32 = mybir.dt.uint32
U8 = mybir.dt.uint8
FP8X4 = mybir.dt.float8_e4m3fn_x4
FP4X4 = mybir.dt.float4_e2m1fn_x4

P = 128
BATCH, SEQ, DIM = 4, 1024, 1024
HEADS, WIDTH = 4, 128
STEPS = BATCH * SEQ // P
CHUNKS = SEQ // STEPS
PACK = 4
K_PASS = P * PACK
HALVES = DIM // K_PASS
WORDS = K_PASS // 2
ROUND = 4
N_ROUNDS = STEPS // ROUND
WARM_FIRST = 3
FIRST_SORTED = 2
TAPS = 7
FP4_BYTES = 2 * WIDTH

FLOPS = 2 * BATCH * SEQ * DIM * WIDTH * TAPS


def load_scale_rows(nc, planes, scales):
    rows = scales.rearrange("a q n -> q a n")
    for quadrant in range(4):
        nc.sync.dma_start(
            out=planes[32 * quadrant : 32 * quadrant + 4].bitcast(I32),
            in_=rows[4 * quadrant : 4 * quadrant + 4].bitcast(I32),
        )


def tile_multiheadhomogeneousattention_pa_t_e_kernel(
    tc, x, w_now_words, w_now_scales, w_back1_words, w_back1_scales, w_back2_words, w_back2_scales, bias, out
):
    nc = tc.nc
    x_chunks = x.rearrange("n (c r) k -> c n (r k)", r=STEPS)
    y_chunks = out.rearrange("n h (c r) q -> h c n (r q)", r=STEPS)

    with ExitStack() as ctx:
        ctx.enter_context(tc.manual_schedule())
        consts = ctx.enter_context(tc.tile_pool(name="consts", bufs=1))
        x_pool = ctx.enter_context(tc.tile_pool(name="x", bufs=1))
        sorted_pool = ctx.enter_context(tc.tile_pool(name="sorted", bufs=2))
        grouped_pool = ctx.enter_context(tc.tile_pool(name="grouped", bufs=3))
        quant_pool = ctx.enter_context(tc.tile_pool(name="quant", bufs=N_ROUNDS))
        y_pool = ctx.enter_context(tc.tile_pool(name="y", bufs=3))
        flip_pool = ctx.enter_context(tc.psum_pool(name="flip", bufs=ROUND))
        acc_pool = ctx.enter_context(tc.psum_pool(name="acc", bufs=ROUND))

        x_words = {}
        x_rounds = {}

        def load_x(queue, i):
            x_round = x_pool.tile([P, ROUND, DIM], BF16, name="x%d" % i, align_bytes=1024)
            queue.dma_start(
                out=x_round[:].rearrange("p j k -> p (j k)"),
                in_=x_chunks[:, :, i * ROUND * DIM : (i + 1) * ROUND * DIM],
            )
            x_rounds[i] = x_round
            for j in range(ROUND):
                x_words[i * ROUND + j] = x_round[:, j, :].bitcast(F32)

        def load_x_in_halves(queue, i):
            for first in (i * ROUND, i * ROUND + 2):
                x_half = x_pool.tile([P, 2, DIM], BF16, name="xh%d" % first, align_bytes=1024)
                queue.dma_start(
                    out=x_half[:].rearrange("p j k -> p (j k)"), in_=x_chunks[:, :, first * DIM : (first + 2) * DIM]
                )
                for j in range(2):
                    x_words[first + j] = x_half[:, j, :].bitcast(F32)

        zeros = consts.tile([P, HEADS * WIDTH], BF16)
        nc.vector.memset(zeros[:], 0.0)
        planes = consts.tile([P, 14, WIDTH], U8, align_bytes=1024)
        nc.vector.memset(planes[:].bitcast(I32), 0)
        back1_planes = planes[:, 8:12, :]
        back2_planes = planes[:, 12:14, :]

        load_x_in_halves(nc.sync, 0)

        bias_bank = acc_pool.tile([P, HEADS, WIDTH], F32, tag="acc")

        def idle_matmuls(count):
            for idle in range(count):
                nc.tensor.matmul(
                    out=bias_bank[:].rearrange("p h q -> p (h q)"), lhsT=zeros[:, 0:P], rhs=zeros[:], start=True, stop=True
                )

        idle_matmuls(WARM_FIRST)
        identity = consts.tile([P, P], F32, align_bytes=1024)
        make_identity(nc, identity[:])
        load_x_in_halves(nc.gpsimd, 1)

        bias_rows = consts.tile([P, HEADS * WIDTH], BF16)
        nc.vector.memset(bias_rows[:], 0.0)
        nc.gpsimd.dma_start(out=bias_rows[0:1, :], in_=bias.rearrange("h q -> (h q)").unsqueeze(0))
        load_x(nc.gpsimd, 2)
        ones = consts.tile([P, P], BF16)
        nc.vector.memset(ones[:], 1.0)

        table_warmer = consts.tile([P, 1], BF16)
        nc.scalar.copy(out=table_warmer[:], in_=ones[:, 0:1])

        now_words_raw = consts.tile([P, HEADS * HALVES, FP4_BYTES], U8, align_bytes=1024)
        now_words = consts.tile([P, HALVES, HEADS, FP4_BYTES], U8, align_bytes=1024)
        now_planes = consts.tile([P, HALVES, HEADS, WIDTH], U8, align_bytes=1024)
        back1_words = consts.tile([P, 2 * HALVES, FP4_BYTES], U8, align_bytes=1024)
        back2_words = consts.tile([P, HALVES, FP4_BYTES], U8, align_bytes=1024)

        load_scale_rows(nc, planes[:, 0:8, :], w_now_scales)
        nc.sync.dma_start(out=now_words_raw[:].bitcast(I32), in_=w_now_words.rearrange("a p b -> p a b").bitcast(I32))
        nc.sync.dma_start(out=back1_words[:].bitcast(I32), in_=w_back1_words.rearrange("a p b -> p a b").bitcast(I32))
        nc.sync.dma_start(out=back2_words[:].bitcast(I32), in_=w_back2_words.rearrange("a p b -> p a b").bitcast(I32))
        load_scale_rows(nc, back1_planes, w_back1_scales)
        load_scale_rows(nc, back2_planes, w_back2_scales)
        for i in range(3, N_ROUNDS):
            load_x(nc.sync, i)

        nc.vector.tensor_copy(
            out=now_words[:].bitcast(I32),
            in_=now_words_raw[:].bitcast(I32).rearrange("p (e g) w -> p g e w", g=HALVES),
        )
        nc.vector.tensor_copy(
            out=now_planes[:].bitcast(I32),
            in_=planes[:, 0:8, :].bitcast(I32).rearrange("p (e g) w -> p g e w", g=HALVES),
        )

        moved_grouped = consts.tile([P, 2, HALVES, P, PACK], BF16, align_bytes=1024)
        moved_codes = consts.tile([P, 2, HALVES * P], U32, align_bytes=1024)
        moved_scales = consts.tile([P, 2, HALVES * P], U8, align_bytes=1024)

        x_codes = {}
        x_scales = {}

        def quantise(step, grouped, codes, scales):
            nc.vector.quantize_mx(
                out=codes.bitcast(FP8X4), scales=scales, in_=grouped.rearrange("p g m t -> p (g m t)")
            )
            x_codes[step] = codes
            x_scales[step] = scales

        sorted_words = {}
        in_order = {}
        by_u = {}
        SCALAR_SHARE = ROUND * HALVES // 2

        def sort_on_scalar(i):
            sorted_round = sorted_pool.tile([P, ROUND * HALVES, 2, P], F32, align_bytes=1024)
            in_order[i] = sorted_round
            as_loaded = x_rounds[i][:].rearrange("p j k -> p (j k)").bitcast(F32)
            by_u[i] = as_loaded.rearrange("p (a q u) -> p a u q", q=P, u=2)
            nc.scalar.copy(out=sorted_round[:, 0:SCALAR_SHARE], in_=by_u[i][:, 0:SCALAR_SHARE])
            for j in range(ROUND):
                sorted_words[i * ROUND + j] = sorted_round[:, HALVES * j : HALVES * (j + 1)]

        def sort_on_vector(i):
            nc.vector.tensor_copy(out=in_order[i][:, SCALAR_SHARE:], in_=by_u[i][:, SCALAR_SHARE:])

        flipped = {}
        grouped = {}
        code_slots = {}
        scale_slots = {}

        def transpose_round(i, in_the_middle=None):
            grouped_round = grouped_pool.tile([P, ROUND, HALVES, P, PACK], BF16, align_bytes=1024)
            codes = quant_pool.tile([P, ROUND, HALVES * P], U32, align_bytes=1024)
            scales = quant_pool.tile([P, ROUND, HALVES * P], U8, align_bytes=1024)
            for j in range(ROUND):
                step = i * ROUND + j
                if j == 2 and in_the_middle:
                    in_the_middle()
                bank = flip_pool.tile([P, HALVES, 2, P], F32)
                flipped[step] = bank
                grouped[step] = grouped_round[:, j]
                code_slots[step] = codes[:, j, :]
                scale_slots[step] = scales[:, j, :]
                for g in range(HALVES):
                    for u in range(2):
                        if i >= FIRST_SORTED:
                            every_second_word = sorted_words[step][:, g, u, :]
                        else:
                            every_second_word = x_words[step][:, WORDS * g + u : WORDS * (g + 1) : 2]
                        nc.tensor.transpose(bank[:, g, u, :], every_second_word, identity[:])

        def pair_words(step):
            paired = flipped[step][:].rearrange("p g u m -> p g m u")
            nc.scalar.copy(out=grouped[step].bitcast(F32), in_=paired)
            if step >= STEPS - 2:
                late = step - (STEPS - 2)
                nc.scalar.copy(
                    out=moved_grouped[:, late, :, BATCH:P, :].bitcast(F32), in_=paired[:, :, 0 : P - BATCH, :]
                )

        def quantise_step(step):
            quantise(step, grouped[step], code_slots[step], scale_slots[step])
            if step >= STEPS - 2:
                late = step - (STEPS - 2)
                quantise(step - STEPS, moved_grouped[:, late], moved_codes[:, late, :], moved_scales[:, late, :])

        def mx_pass(acc, step, g, words, plane, start, stop):
            token_cols = slice(g * P, (g + 1) * P)
            nc.tensor.matmul_mx(
                out=acc,
                lhsT=x_codes[step][:, token_cols].bitcast(FP8X4),
                lhsT_scale=x_scales[step][:, token_cols],
                rhs=words.bitcast(FP4X4),
                rhs_scale=plane,
                start=start,
                stop=stop,
            )

        def multiply_step(y_round, j, step):
            acc = acc_pool.tile([P, HEADS, WIDTH], F32)
            everything = acc[:].rearrange("p h q -> p (h q)")
            mx_pass(
                everything, step, 0, now_words[:, 0].rearrange("p e b -> p (e b)"),
                now_planes[:, 0].rearrange("p e n -> p (e n)"), True, False,
            )
            for g in range(HALVES):
                for e in range(2):
                    mx_pass(
                        acc[:, 2 + e, :], step - 1, g, back1_words[:, HALVES * e + g, :],
                        back1_planes[:, HALVES * e + g, :], False, False,
                    )
            for g in range(HALVES):
                mx_pass(acc[:, 3, :], step - 2, g, back2_words[:, g, :], back2_planes[:, g, :], False, False)
            mx_pass(
                everything, step, 1, now_words[:, 1].rearrange("p e b -> p (e b)"),
                now_planes[:, 1].rearrange("p e n -> p (e n)"), False, True,
            )
            nc.vector.tensor_tensor(out=y_round[:, :, j, :], in0=acc[:], in1=bias_all[:], op=mybir.AluOpType.add)

        def store(y_round, first, count):
            for h in range(HEADS):
                nc.sync.dma_start(
                    out=y_chunks[h, :, :, first * WIDTH : (first + count) * WIDTH],
                    in_=y_round[:, h].rearrange("p j q -> p (j q)"),
                )

        bias_all = consts.tile([P, HEADS, WIDTH], F32, align_bytes=1024)
        def spread_bias():
            nc.tensor.matmul(
                out=bias_bank[:].rearrange("p h q -> p (h q)"), lhsT=ones[:], rhs=bias_rows[:], start=True, stop=True
            )

        for i in range(2):
            transpose_round(i, spread_bias if i == 1 else None)
            for j in range(ROUND):
                pair_words(i * ROUND + j)
                quantise_step(i * ROUND + j)
            if i == 1:
                nc.vector.tensor_copy(out=bias_all[:], in_=bias_bank[:])
        sort_on_scalar(FIRST_SORTED)
        sort_on_vector(FIRST_SORTED)
        nc.vector.memset(moved_grouped[:], 0.0)

        y_round = y_pool.tile([P, HEADS, 2, WIDTH], F32, align_bytes=1024)
        for j in range(2):
            multiply_step(y_round, j, 2 + j)
        store(y_round, 2, 2)

        for i in range(1, N_ROUNDS):
            ahead = i + 1
            to_sort = i + 2
            first = i * ROUND
            y_round = y_pool.tile([P, HEADS, ROUND, WIDTH], F32, align_bytes=1024)
            if ahead < N_ROUNDS:
                transpose_round(ahead)
                for j in range(ROUND):
                    pair_words(ahead * ROUND + j)
            if to_sort < N_ROUNDS:
                sort_on_scalar(to_sort)
            if ahead < N_ROUNDS:
                quantise_step(ahead * ROUND)
                quantise_step(ahead * ROUND + 1)
            multiply_step(y_round, 0, first)
            if ahead < N_ROUNDS:
                quantise_step(ahead * ROUND + 2)
            multiply_step(y_round, 1, first + 1)
            if ahead < N_ROUNDS:
                quantise_step(ahead * ROUND + 3)
            if to_sort < N_ROUNDS:
                sort_on_vector(to_sort)
            multiply_step(y_round, 2, first + 2)
            multiply_step(y_round, 3, first + 3)
            store(y_round, first, ROUND)

        y_round = y_pool.tile([P, HEADS, 2, WIDTH], F32, align_bytes=1024)
        for j in range(2):
            multiply_step(y_round, j, j)
        store(y_round, 0, 2)
